import numpy as np
import ml_dtypes


def mxq(x, axis, fmt="e4m3"):
    dtype, down = {"e4m3": (ml_dtypes.float8_e4m3fn, 7), "e5m2": (ml_dtypes.float8_e5m2, 14)}[fmt]
    v = np.moveaxis(np.asarray(x, np.float32).astype(ml_dtypes.bfloat16).astype(np.float64), axis, -1)
    blocks = v.reshape(v.shape[:-1] + (-1, 32))
    amax = np.abs(blocks).max(-1, keepdims=True)
    byte = np.maximum(np.where(amax > 0, np.frexp(amax)[1] - 1 + 127, 0) - down, 1)
    scale = np.exp2(byte - 127.0)
    codes = (blocks / scale).astype(np.float32).astype(dtype).astype(np.float64)
    return np.moveaxis((codes * scale).reshape(v.shape), -1, axis)


WIDE = False


def mx_kscale(k):
    if not WIDE:
        return np.ones(k)
    levels = np.array([20, -20, 10, -10, 0])
    a = np.random.permutation(np.resize(levels, k // 512 * 4)).reshape(k // 512, 4)
    idx = np.arange(k)
    return np.exp2(a[idx // 512, idx % 128 // 32])


BF16 = ml_dtypes.bfloat16


def bf(x):
    return np.asarray(x, np.float32).astype(BF16)


def f64(x):
    return np.asarray(x).astype(np.float64)


B, C, K, BK, BN = 512, 2048, 2048, 1, 16
KEEP = 0.3


def setup_inputs():
    s = mx_kscale(B)[:, None]
    x0 = bf(np.random.standard_normal((B, C)))
    weight = np.random.uniform(-1.0, 1.0, (K, C)) * 3.2 / np.sqrt(C)
    blk = (np.random.uniform(0.0, 1.0, (K // BK, C // BN)) < KEEP).astype(np.float64)
    mask = np.repeat(np.repeat(blk, BK, axis=0), BN, axis=1)
    weight = bf(weight * mask)
    bias = bf(np.random.uniform(-1.0, 1.0, K) * 0.5)
    g = bf(np.random.standard_normal((B, K)) * np.exp2(np.random.randint(-12, 1, (B, 1))) / s)
    z = f64(x0) @ f64(weight).T + f64(bias)
    return {"x": bf(f64(x0) * s), "weight": weight, "bias": bias, "z": np.asarray(z, np.float32), "grad_out": g}


def reference(x, weight, bias, z, grad_out):
    dz = f64(grad_out) * (f64(z) > 0.0)
    return mxq(dz, 0, "e5m2").T @ mxq(f64(x), 0, "e4m3")

@@ -1,0 +1,125 @@
+from contextlib import ExitStack
+
+import concourse.mybir as mybir
+
+F32 = mybir.dt.float32
+BF16 = mybir.dt.bfloat16
+U32 = mybir.dt.uint32
+U8 = mybir.dt.uint8
+E4M3_X4 = mybir.dt.float8_e4m3fn_x4
+E5M2_X4 = mybir.dt.float8_e5m2_x4
+ALU = mybir.AluOpType
+
+P = 128
+PACK = 4
+TOKENS = P * PACK
+F_OUT = 2048
+F_IN = 2048
+
+M_TILE = 128
+N_TILE = 512
+N_TILES = F_IN // N_TILE
+
+LOAD_COLS = 1024
+STEP_COLS = 256
+STEPS = F_OUT // STEP_COLS
+STEPS_PER_LOAD = LOAD_COLS // STEP_COLS
+M_TILES_PER_STEP = STEP_COLS // M_TILE
+
+OUT_BUFS = 8
+
+FLOPS = 2 * TOKENS * F_OUT * F_IN
+BYTES = TOKENS * F_IN * 2 + TOKENS * F_OUT * 2 + TOKENS * F_OUT * 4 + F_OUT * F_IN * 4
+
+
+def tile_sparselinearrelu_v_kernel(tc, x, weight, bias, z, grad_out, out):
+    nc = tc.nc
+    with ExitStack() as ctx:
+        keep = ctx.enter_context(tc.tile_pool(name="keep", bufs=1))
+        stage = ctx.enter_context(tc.tile_pool(name="stage", bufs=3))
+        done = ctx.enter_context(tc.tile_pool(name="done", bufs=OUT_BUFS))
+        psum = ctx.enter_context(tc.psum_pool(name="psum", bufs=8))
+
+        x_rows = keep.tile([P, PACK, F_IN], BF16)
+        nc.sync.dma_start(out=x_rows[:], in_=x.rearrange("(p j) f -> p j f", j=PACK))
+        z_by_token = z.rearrange("(p j) f -> p j f", j=PACK)
+        g_by_token = grad_out.rearrange("(p j) f -> p j f", j=PACK)
+        z_rows = []
+        g_rows = []
+        for h in range(F_OUT // LOAD_COLS):
+            load_cols = slice(h * LOAD_COLS, (h + 1) * LOAD_COLS)
+            z_part = keep.tile([P, PACK, LOAD_COLS], F32, name="z_rows%d" % h)
+            nc.sync.dma_start(out=z_part[:], in_=z_by_token[:, :, load_cols])
+            g_part = keep.tile([P, PACK, LOAD_COLS], BF16, name="g_rows%d" % h)
+            nc.sync.dma_start(out=g_part[:], in_=g_by_token[:, :, load_cols])
+            z_rows.append(z_part)
+            g_rows.append(g_part)
+
+        x_codes = keep.tile([P, F_IN], U32, align_bytes=64)
+        x_scales = keep.tile([P, F_IN], U8, align_bytes=64)
+        x_grouped = []
+        for n in range(N_TILES):
+            n_cols = slice(n * N_TILE, (n + 1) * N_TILE)
+            grouped = keep.tile([P, N_TILE, PACK], BF16, name="x_grouped%d" % n, align_bytes=64)
+            nc.vector.tensor_copy(
+                out=grouped[:].rearrange("p (c i) j -> p c j i", i=4),
+                in_=x_rows[:, :, n_cols].rearrange("p j (c i) -> p c j i", i=4),
+            )
+            x_grouped.append(grouped)
+        for n in range(N_TILES):
+            n_cols = slice(n * N_TILE, (n + 1) * N_TILE)
+            nc.vector.quantize_mx(
+                out=x_codes[:, n_cols].bitcast(E4M3_X4),
+                scales=x_scales[:, n_cols],
+                in_=x_grouped[n][:].rearrange("p f j -> p (f j)"),
+            )
+
+        dz_codes = keep.tile([P, F_OUT], U32, align_bytes=64)
+        dz_scales = keep.tile([P, F_OUT], U8, align_bytes=64)
+
+        def prepare_dz(s):
+            h = s // STEPS_PER_LOAD
+            part_cols = slice((s % STEPS_PER_LOAD) * STEP_COLS, (s % STEPS_PER_LOAD + 1) * STEP_COLS)
+            step_cols = slice(s * STEP_COLS, (s + 1) * STEP_COLS)
+            dz_grouped = stage.tile([P, STEP_COLS, PACK], BF16, align_bytes=64)
+            nc.vector.scalar_tensor_tensor(
+                out=dz_grouped[:],
+                in0=z_rows[h][:, :, part_cols].rearrange("p j f -> p f j"),
+                scalar=0.0,
+                in1=g_rows[h][:, :, part_cols].rearrange("p j f -> p f j"),
+                op0=ALU.is_gt,
+                op1=ALU.mult,
+            )
+            nc.vector.quantize_mx(
+                out=dz_codes[:, step_cols].bitcast(E5M2_X4),
+                scales=dz_scales[:, step_cols],
+                in_=dz_grouped[:].rearrange("p f j -> p (f j)"),
+            )
+
+        def multiply_and_store(m):
+            m_cols = slice(m * M_TILE, (m + 1) * M_TILE)
+            out_rows = done.tile([P, F_IN], F32)
+            for n in range(N_TILES):
+                n_cols = slice(n * N_TILE, (n + 1) * N_TILE)
+                acc = psum.tile([P, N_TILE], F32)
+                nc.tensor.matmul_mx(
+                    out=acc[:],
+                    lhsT=dz_codes[:, m_cols].bitcast(E5M2_X4),
+                    lhsT_scale=dz_scales[:, m_cols],
+                    rhs=x_codes[:, n_cols].bitcast(E4M3_X4),
+                    rhs_scale=x_scales[:, n_cols],
+                    start=True,
+                    stop=True,
+                )
+                if n == N_TILES - 1:
+                    nc.vector.tensor_copy(out=out_rows[:, n_cols], in_=acc[:])
+                else:
+                    nc.scalar.copy(out=out_rows[:, n_cols], in_=acc[:])
+            nc.sync.dma_start(out=out[m_cols, :], in_=out_rows[:])
+
+        prepare_dz(0)
+        for s in range(STEPS):
+            if s + 1 < STEPS:
+                prepare_dz(s + 1)
+            for a in range(M_TILES_PER_STEP):
+                multiply_and_store(s * M_TILES_PER_STEP + a)

@@ -20,10 +20,9 @@ M_TILE = 128
 N_TILE = 512
 N_TILES = F_IN // N_TILE
 
-LOAD_COLS = 1024
+FIRST_LOAD_COLS = 512
 STEP_COLS = 256
 STEPS = F_OUT // STEP_COLS
-STEPS_PER_LOAD = LOAD_COLS // STEP_COLS
 M_TILES_PER_STEP = STEP_COLS // M_TILE
 
 OUT_BUFS = 8
@@ -44,13 +43,16 @@ def tile_sparselinearrelu_v_kernel(tc, x, weight, bias, z, grad_out, out):
         nc.sync.dma_start(out=x_rows[:], in_=x.rearrange("(p j) f -> p j f", j=PACK))
         z_by_token = z.rearrange("(p j) f -> p j f", j=PACK)
         g_by_token = grad_out.rearrange("(p j) f -> p j f", j=PACK)
+        part_starts = (0, FIRST_LOAD_COLS)
+        part_ends = (FIRST_LOAD_COLS, F_OUT)
         z_rows = []
         g_rows = []
-        for h in range(F_OUT // LOAD_COLS):
-            load_cols = slice(h * LOAD_COLS, (h + 1) * LOAD_COLS)
-            z_part = keep.tile([P, PACK, LOAD_COLS], F32, name="z_rows%d" % h)
+        for h in range(2):
+            load_cols = slice(part_starts[h], part_ends[h])
+            width = part_ends[h] - part_starts[h]
+            z_part = keep.tile([P, PACK, width], F32, name="z_rows%d" % h)
             nc.sync.dma_start(out=z_part[:], in_=z_by_token[:, :, load_cols])
-            g_part = keep.tile([P, PACK, LOAD_COLS], BF16, name="g_rows%d" % h)
+            g_part = keep.tile([P, PACK, width], BF16, name="g_rows%d" % h)
             nc.sync.dma_start(out=g_part[:], in_=g_by_token[:, :, load_cols])
             z_rows.append(z_part)
             g_rows.append(g_part)
@@ -61,10 +63,12 @@ def tile_sparselinearrelu_v_kernel(tc, x, weight, bias, z, grad_out, out):
         for n in range(N_TILES):
             n_cols = slice(n * N_TILE, (n + 1) * N_TILE)
             grouped = keep.tile([P, N_TILE, PACK], BF16, name="x_grouped%d" % n, align_bytes=64)
-            nc.vector.tensor_copy(
-                out=grouped[:].rearrange("p (c i) j -> p c j i", i=4),
-                in_=x_rows[:, :, n_cols].rearrange("p j (c i) -> p c j i", i=4),
-            )
+            by_feature = grouped[:].rearrange("p (c i) j -> p c j i", i=4)
+            by_token = x_rows[:, :, n_cols].rearrange("p j (c i) -> p c j i", i=4)
+            if n % 2 == 0:
+                nc.vector.tensor_copy(out=by_feature, in_=by_token)
+            else:
+                nc.scalar.copy(out=by_feature, in_=by_token)
             x_grouped.append(grouped)
         for n in range(N_TILES):
             n_cols = slice(n * N_TILE, (n + 1) * N_TILE)
@@ -78,9 +82,9 @@ def tile_sparselinearrelu_v_kernel(tc, x, weight, bias, z, grad_out, out):
         dz_scales = keep.tile([P, F_OUT], U8, align_bytes=64)
 
         def prepare_dz(s):
-            h = s // STEPS_PER_LOAD
-            part_cols = slice((s % STEPS_PER_LOAD) * STEP_COLS, (s % STEPS_PER_LOAD + 1) * STEP_COLS)
             step_cols = slice(s * STEP_COLS, (s + 1) * STEP_COLS)
+            h = 0 if s * STEP_COLS < FIRST_LOAD_COLS else 1
+            part_cols = slice(s * STEP_COLS - part_starts[h], (s + 1) * STEP_COLS - part_starts[h])
             dz_grouped = stage.tile([P, STEP_COLS, PACK], BF16, align_bytes=64)
             nc.vector.scalar_tensor_tensor(
                 out=dz_grouped[:],

@@ -20,7 +20,7 @@ M_TILE = 128
 N_TILE = 512
 N_TILES = F_IN // N_TILE
 
-FIRST_LOAD_COLS = 512
+FIRST_LOAD_COLS = 768
 STEP_COLS = 256
 STEPS = F_OUT // STEP_COLS
 M_TILES_PER_STEP = STEP_COLS // M_TILE

@@ -25,6 +25,7 @@ STEP_COLS = 256
 STEPS = F_OUT // STEP_COLS
 M_TILES_PER_STEP = STEP_COLS // M_TILE
 
+DMA_ALIGN = 256
 OUT_BUFS = 8
 
 FLOPS = 2 * TOKENS * F_OUT * F_IN
@@ -39,7 +40,7 @@ def tile_sparselinearrelu_v_kernel(tc, x, weight, bias, z, grad_out, out):
         done = ctx.enter_context(tc.tile_pool(name="done", bufs=OUT_BUFS))
         psum = ctx.enter_context(tc.psum_pool(name="psum", bufs=8))
 
-        x_rows = keep.tile([P, PACK, F_IN], BF16)
+        x_rows = keep.tile([P, PACK, F_IN], BF16, align_bytes=DMA_ALIGN)
         nc.sync.dma_start(out=x_rows[:], in_=x.rearrange("(p j) f -> p j f", j=PACK))
         z_by_token = z.rearrange("(p j) f -> p j f", j=PACK)
         g_by_token = grad_out.rearrange("(p j) f -> p j f", j=PACK)
@@ -50,9 +51,9 @@ def tile_sparselinearrelu_v_kernel(tc, x, weight, bias, z, grad_out, out):
         for h in range(2):
             load_cols = slice(part_starts[h], part_ends[h])
             width = part_ends[h] - part_starts[h]
-            z_part = keep.tile([P, PACK, width], F32, name="z_rows%d" % h)
+            z_part = keep.tile([P, PACK, width], F32, name="z_rows%d" % h, align_bytes=DMA_ALIGN)
             nc.sync.dma_start(out=z_part[:], in_=z_by_token[:, :, load_cols])
-            g_part = keep.tile([P, PACK, width], BF16, name="g_rows%d" % h)
+            g_part = keep.tile([P, PACK, width], BF16, name="g_rows%d" % h, align_bytes=DMA_ALIGN)
             nc.sync.dma_start(out=g_part[:], in_=g_by_token[:, :, load_cols])
             z_rows.append(z_part)
             g_rows.append(g_part)
@@ -102,7 +103,7 @@ def tile_sparselinearrelu_v_kernel(tc, x, weight, bias, z, grad_out, out):
 
         def multiply_and_store(m):
             m_cols = slice(m * M_TILE, (m + 1) * M_TILE)
-            out_rows = done.tile([P, F_IN], F32)
+            out_rows = done.tile([P, F_IN], F32, align_bytes=DMA_ALIGN)
             for n in range(N_TILES):
                 n_cols = slice(n * N_TILE, (n + 1) * N_TILE)
                 acc = psum.tile([P, N_TILE], F32)

@@ -20,7 +20,8 @@ M_TILE = 128
 N_TILE = 512
 N_TILES = F_IN // N_TILE
 
-FIRST_LOAD_COLS = 768
+Z_FIRST_LOAD_COLS = 512
+G_FIRST_LOAD_COLS = 1024
 STEP_COLS = 256
 STEPS = F_OUT // STEP_COLS
 M_TILES_PER_STEP = STEP_COLS // M_TILE
@@ -44,19 +45,23 @@ def tile_sparselinearrelu_v_kernel(tc, x, weight, bias, z, grad_out, out):
         nc.sync.dma_start(out=x_rows[:], in_=x.rearrange("(p j) f -> p j f", j=PACK))
         z_by_token = z.rearrange("(p j) f -> p j f", j=PACK)
         g_by_token = grad_out.rearrange("(p j) f -> p j f", j=PACK)
-        part_starts = (0, FIRST_LOAD_COLS)
-        part_ends = (FIRST_LOAD_COLS, F_OUT)
-        z_rows = []
-        g_rows = []
-        for h in range(2):
-            load_cols = slice(part_starts[h], part_ends[h])
-            width = part_ends[h] - part_starts[h]
-            z_part = keep.tile([P, PACK, width], F32, name="z_rows%d" % h, align_bytes=DMA_ALIGN)
-            nc.sync.dma_start(out=z_part[:], in_=z_by_token[:, :, load_cols])
-            g_part = keep.tile([P, PACK, width], BF16, name="g_rows%d" % h, align_bytes=DMA_ALIGN)
-            nc.sync.dma_start(out=g_part[:], in_=g_by_token[:, :, load_cols])
-            z_rows.append(z_part)
-            g_rows.append(g_part)
+
+        def load_part(by_token, dtype, name, first_col, end_col):
+            part = keep.tile([P, PACK, end_col - first_col], dtype, name=name, align_bytes=DMA_ALIGN)
+            nc.sync.dma_start(out=part[:], in_=by_token[:, :, first_col:end_col])
+            return part
+
+        g0 = load_part(g_by_token, BF16, "g_rows0", 0, G_FIRST_LOAD_COLS)
+        z0 = load_part(z_by_token, F32, "z_rows0", 0, Z_FIRST_LOAD_COLS)
+        z1 = load_part(z_by_token, F32, "z_rows1", Z_FIRST_LOAD_COLS, F_OUT)
+        g1 = load_part(g_by_token, BF16, "g_rows1", G_FIRST_LOAD_COLS, F_OUT)
+        z_rows = (z0, z1)
+        g_rows = (g0, g1)
+
+        def columns_of(parts, first_load_cols, first_col):
+            h = 0 if first_col < first_load_cols else 1
+            local = first_col - h * first_load_cols
+            return parts[h][:, :, local : local + STEP_COLS].rearrange("p j f -> p f j")
 
         x_codes = keep.tile([P, F_IN], U32, align_bytes=64)
         x_scales = keep.tile([P, F_IN], U8, align_bytes=64)
@@ -71,7 +76,8 @@ def tile_sparselinearrelu_v_kernel(tc, x, weight, bias, z, grad_out, out):
             else:
                 nc.scalar.copy(out=by_feature, in_=by_token)
             x_grouped.append(grouped)
-        for n in range(N_TILES):
+
+        def quantise_x(n):
             n_cols = slice(n * N_TILE, (n + 1) * N_TILE)
             nc.vector.quantize_mx(
                 out=x_codes[:, n_cols].bitcast(E4M3_X4),
@@ -82,19 +88,20 @@ def tile_sparselinearrelu_v_kernel(tc, x, weight, bias, z, grad_out, out):
         dz_codes = keep.tile([P, F_OUT], U32, align_bytes=64)
         dz_scales = keep.tile([P, F_OUT], U8, align_bytes=64)
 
-        def prepare_dz(s):
-            step_cols = slice(s * STEP_COLS, (s + 1) * STEP_COLS)
-            h = 0 if s * STEP_COLS < FIRST_LOAD_COLS else 1
-            part_cols = slice(s * STEP_COLS - part_starts[h], (s + 1) * STEP_COLS - part_starts[h])
+        def mask_dz(s):
             dz_grouped = stage.tile([P, STEP_COLS, PACK], BF16, align_bytes=64)
             nc.vector.scalar_tensor_tensor(
                 out=dz_grouped[:],
-                in0=z_rows[h][:, :, part_cols].rearrange("p j f -> p f j"),
+                in0=columns_of(z_rows, Z_FIRST_LOAD_COLS, s * STEP_COLS),
                 scalar=0.0,
-                in1=g_rows[h][:, :, part_cols].rearrange("p j f -> p f j"),
+                in1=columns_of(g_rows, G_FIRST_LOAD_COLS, s * STEP_COLS),
                 op0=ALU.is_gt,
                 op1=ALU.mult,
             )
+            return dz_grouped
+
+        def quantise_dz(s, dz_grouped):
+            step_cols = slice(s * STEP_COLS, (s + 1) * STEP_COLS)
             nc.vector.quantize_mx(
                 out=dz_codes[:, step_cols].bitcast(E5M2_X4),
                 scales=dz_scales[:, step_cols],
@@ -122,9 +129,16 @@ def tile_sparselinearrelu_v_kernel(tc, x, weight, bias, z, grad_out, out):
                     nc.scalar.copy(out=out_rows[:, n_cols], in_=acc[:])
             nc.sync.dma_start(out=out[m_cols, :], in_=out_rows[:])
 
-        prepare_dz(0)
+        for n in range(N_TILES - 1):
+            quantise_x(n)
+        first_dz = mask_dz(0)
+        quantise_x(N_TILES - 1)
+        quantise_dz(0, first_dz)
         for s in range(STEPS):
-            if s + 1 < STEPS:
-                prepare_dz(s + 1)
+            next_waits_for_load = (s + 1) * STEP_COLS == Z_FIRST_LOAD_COLS
+            if s + 1 < STEPS and not next_waits_for_load:
+                quantise_dz(s + 1, mask_dz(s + 1))
             for a in range(M_TILES_PER_STEP):
                 multiply_and_store(s * M_TILES_PER_STEP + a)
+            if next_waits_for_load:
+                quantise_dz(s + 1, mask_dz(s + 1))

@@ -40,6 +40,7 @@ def tile_sparselinearrelu_v_kernel(tc, x, weight, bias, z, grad_out, out):
         stage = ctx.enter_context(tc.tile_pool(name="stage", bufs=3))
         done = ctx.enter_context(tc.tile_pool(name="done", bufs=OUT_BUFS))
         psum = ctx.enter_context(tc.psum_pool(name="psum", bufs=8))
+        ctx.enter_context(tc.manual_schedule())
 
         x_rows = keep.tile([P, PACK, F_IN], BF16, align_bytes=DMA_ALIGN)
         nc.sync.dma_start(out=x_rows[:], in_=x.rearrange("(p j) f -> p j f", j=PACK))
@@ -131,14 +132,12 @@ def tile_sparselinearrelu_v_kernel(tc, x, weight, bias, z, grad_out, out):
 
         for n in range(N_TILES - 1):
             quantise_x(n)
-        first_dz = mask_dz(0)
+        quantise_dz(0, mask_dz(0))
         quantise_x(N_TILES - 1)
-        quantise_dz(0, first_dz)
         for s in range(STEPS):
-            next_waits_for_load = (s + 1) * STEP_COLS == Z_FIRST_LOAD_COLS
-            if s + 1 < STEPS and not next_waits_for_load:
-                quantise_dz(s + 1, mask_dz(s + 1))
-            for a in range(M_TILES_PER_STEP):
-                multiply_and_store(s * M_TILES_PER_STEP + a)
-            if next_waits_for_load:
-                quantise_dz(s + 1, mask_dz(s + 1))
+            if s + 1 < STEPS:
+                next_dz = mask_dz(s + 1)
+            multiply_and_store(s * M_TILES_PER_STEP)
+            if s + 1 < STEPS:
+                quantise_dz(s + 1, next_dz)
+            multiply_and_store(s * M_TILES_PER_STEP + 1)

from contextlib import ExitStack

import concourse.mybir as mybir

F32 = mybir.dt.float32
BF16 = mybir.dt.bfloat16
U32 = mybir.dt.uint32
U8 = mybir.dt.uint8
E4M3_X4 = mybir.dt.float8_e4m3fn_x4
E5M2_X4 = mybir.dt.float8_e5m2_x4
ALU = mybir.AluOpType

P = 128
PACK = 4
TOKENS = P * PACK
F_OUT = 2048
F_IN = 2048

M_TILE = 128
N_TILE = 512
N_TILES = F_IN // N_TILE

Z_FIRST_LOAD_COLS = 512
G_FIRST_LOAD_COLS = 1024
STEP_COLS = 256
STEPS = F_OUT // STEP_COLS
M_TILES_PER_STEP = STEP_COLS // M_TILE

DMA_ALIGN = 256
OUT_BUFS = 8

FLOPS = 2 * TOKENS * F_OUT * F_IN
BYTES = TOKENS * F_IN * 2 + TOKENS * F_OUT * 2 + TOKENS * F_OUT * 4 + F_OUT * F_IN * 4


def tile_sparselinearrelu_v_kernel(tc, x, weight, bias, z, grad_out, out):
    nc = tc.nc
    with ExitStack() as ctx:
        keep = ctx.enter_context(tc.tile_pool(name="keep", bufs=1))
        stage = ctx.enter_context(tc.tile_pool(name="stage", bufs=3))
        done = ctx.enter_context(tc.tile_pool(name="done", bufs=OUT_BUFS))
        psum = ctx.enter_context(tc.psum_pool(name="psum", bufs=8))
        ctx.enter_context(tc.manual_schedule())

        x_rows = keep.tile([P, PACK, F_IN], BF16, align_bytes=DMA_ALIGN)
        nc.sync.dma_start(out=x_rows[:], in_=x.rearrange("(p j) f -> p j f", j=PACK))
        z_by_token = z.rearrange("(p j) f -> p j f", j=PACK)
        g_by_token = grad_out.rearrange("(p j) f -> p j f", j=PACK)

        def load_part(by_token, dtype, name, first_col, end_col):
            part = keep.tile([P, PACK, end_col - first_col], dtype, name=name, align_bytes=DMA_ALIGN)
            nc.sync.dma_start(out=part[:], in_=by_token[:, :, first_col:end_col])
            return part

        g0 = load_part(g_by_token, BF16, "g_rows0", 0, G_FIRST_LOAD_COLS)
        z0 = load_part(z_by_token, F32, "z_rows0", 0, Z_FIRST_LOAD_COLS)
        z1 = load_part(z_by_token, F32, "z_rows1", Z_FIRST_LOAD_COLS, F_OUT)
        g1 = load_part(g_by_token, BF16, "g_rows1", G_FIRST_LOAD_COLS, F_OUT)
        z_rows = (z0, z1)
        g_rows = (g0, g1)

        def columns_of(parts, first_load_cols, first_col):
            h = 0 if first_col < first_load_cols else 1
            local = first_col - h * first_load_cols
            return parts[h][:, :, local : local + STEP_COLS].rearrange("p j f -> p f j")

        x_codes = keep.tile([P, F_IN], U32, align_bytes=64)
        x_scales = keep.tile([P, F_IN], U8, align_bytes=64)
        x_grouped = []
        for n in range(N_TILES):
            n_cols = slice(n * N_TILE, (n + 1) * N_TILE)
            grouped = keep.tile([P, N_TILE, PACK], BF16, name="x_grouped%d" % n, align_bytes=64)
            by_feature = grouped[:].rearrange("p (c i) j -> p c j i", i=4)
            by_token = x_rows[:, :, n_cols].rearrange("p j (c i) -> p c j i", i=4)
            if n % 2 == 0:
                nc.vector.tensor_copy(out=by_feature, in_=by_token)
            else:
                nc.scalar.copy(out=by_feature, in_=by_token)
            x_grouped.append(grouped)

        def quantise_x(n):
            n_cols = slice(n * N_TILE, (n + 1) * N_TILE)
            nc.vector.quantize_mx(
                out=x_codes[:, n_cols].bitcast(E4M3_X4),
                scales=x_scales[:, n_cols],
                in_=x_grouped[n][:].rearrange("p f j -> p (f j)"),
            )

        dz_codes = keep.tile([P, F_OUT], U32, align_bytes=64)
        dz_scales = keep.tile([P, F_OUT], U8, align_bytes=64)

        def mask_dz(s):
            dz_grouped = stage.tile([P, STEP_COLS, PACK], BF16, align_bytes=64)
            nc.vector.scalar_tensor_tensor(
                out=dz_grouped[:],
                in0=columns_of(z_rows, Z_FIRST_LOAD_COLS, s * STEP_COLS),
                scalar=0.0,
                in1=columns_of(g_rows, G_FIRST_LOAD_COLS, s * STEP_COLS),
                op0=ALU.is_gt,
                op1=ALU.mult,
            )
            return dz_grouped

        def quantise_dz(s, dz_grouped):
            step_cols = slice(s * STEP_COLS, (s + 1) * STEP_COLS)
            nc.vector.quantize_mx(
                out=dz_codes[:, step_cols].bitcast(E5M2_X4),
                scales=dz_scales[:, step_cols],
                in_=dz_grouped[:].rearrange("p f j -> p (f j)"),
            )

        def multiply_and_store(m):
            m_cols = slice(m * M_TILE, (m + 1) * M_TILE)
            out_rows = done.tile([P, F_IN], F32, align_bytes=DMA_ALIGN)
            for n in range(N_TILES):
                n_cols = slice(n * N_TILE, (n + 1) * N_TILE)
                acc = psum.tile([P, N_TILE], F32)
                nc.tensor.matmul_mx(
                    out=acc[:],
                    lhsT=dz_codes[:, m_cols].bitcast(E5M2_X4),
                    lhsT_scale=dz_scales[:, m_cols],
                    rhs=x_codes[:, n_cols].bitcast(E4M3_X4),
                    rhs_scale=x_scales[:, n_cols],
                    start=True,
                    stop=True,
                )
                if n == N_TILES - 1:
                    nc.vector.tensor_copy(out=out_rows[:, n_cols], in_=acc[:])
                else:
                    nc.scalar.copy(out=out_rows[:, n_cols], in_=acc[:])
            nc.sync.dma_start(out=out[m_cols, :], in_=out_rows[:])

        for n in range(N_TILES - 1):
            quantise_x(n)
        quantise_dz(0, mask_dz(0))
        quantise_x(N_TILES - 1)
        for s in range(STEPS):
            if s + 1 < STEPS:
                next_dz = mask_dz(s + 1)
            multiply_and_store(s * M_TILES_PER_STEP)
            if s + 1 < STEPS:
                quantise_dz(s + 1, next_dz)
            multiply_and_store(s * M_TILES_PER_STEP + 1)
